import numpy as np
import ml_dtypes


def mxq(x, axis, fmt="e4m3"):
    dtype, down = {"e4m3": (ml_dtypes.float8_e4m3fn, 7), "e5m2": (ml_dtypes.float8_e5m2, 14)}[fmt]
    v = np.moveaxis(np.asarray(x, np.float32).astype(ml_dtypes.bfloat16).astype(np.float64), axis, -1)
    blocks = v.reshape(v.shape[:-1] + (-1, 32))
    amax = np.abs(blocks).max(-1, keepdims=True)
    byte = np.maximum(np.where(amax > 0, np.frexp(amax)[1] - 1 + 127, 0) - down, 1)
    scale = np.exp2(byte - 127.0)
    codes = (blocks / scale).astype(np.float32).astype(dtype).astype(np.float64)
    return np.moveaxis((codes * scale).reshape(v.shape), -1, axis)


WIDE = False


def mx_kscale(k):
    if not WIDE:
        return np.ones(k)
    levels = np.array([10, -10, 5, -5, 0])
    a = np.random.permutation(np.resize(levels, k // 512 * 4)).reshape(k // 512, 4)
    idx = np.arange(k)
    return np.exp2(a[idx // 512, idx % 128 // 32])


BF16 = ml_dtypes.bfloat16


def bf(x):
    return np.asarray(x, np.float32).astype(BF16)


def f64(x):
    return np.asarray(x).astype(np.float64)


T, K, N = 4096, 512, 1024


def _quantize(W, alpha_eff, bitwidth):
    Wa = W / alpha_eff
    Wc = np.clip(Wa, -1.0, 1.0)
    if bitwidth == 1:
        Q = np.sign(Wc)
        Q = np.where(Q == 0, 1.0, Q)
    elif bitwidth == 2:
        Q = np.where(np.abs(Wc) < 0.5, 0.0, np.sign(Wc))
    else:
        raise ValueError("bitwidth must be 1 or 2 here")
    return alpha_eff * Q


def setup_inputs():
    bound = 2.0 / np.sqrt(K)
    s = mx_kscale(K)
    g = np.maximum(s, 1.0) ** 2
    return {"x": bf(np.random.standard_normal((T, K)) * g[None, :]),
            "weight": bf(np.random.uniform(-bound, bound, (N, K)) / g[None, :]),
            "alpha": bf((1.5 / np.sqrt(K)) * (1.0 + 0.1 * np.random.standard_normal(1))),
            "bias": bf(0.1 * np.random.standard_normal(N)),
            "bitwidth": 2}


def reference(x, weight, alpha, bias, bitwidth):
    if bitwidth == 32:
        W_used = f64(weight)
    else:
        alpha_eff = np.abs(f64(alpha)) + 1e-8
        W_used = _quantize(f64(weight), alpha_eff, bitwidth)
    return (mxq(f64(x), 1, "e4m3") @ mxq(W_used, 1, "e4m3").T) + f64(bias)

@@ -1,0 +1,164 @@
+from contextlib import ExitStack
+
+import concourse.mybir as mybir
+from concourse.masks import make_identity
+
+F32 = mybir.dt.float32
+BF16 = mybir.dt.bfloat16
+U32 = mybir.dt.uint32
+U8 = mybir.dt.uint8
+FP8X4 = mybir.dt.float8_e4m3fn_x4
+ALU = mybir.AluOpType
+
+T, K, N = 4096, 512, 1024
+FLOPS = 2 * T * K * N
+
+P = 128
+PACK = 4
+assert K == P * PACK
+GROUP = 4
+BANK = 512
+TOKEN_TILES = T // P
+ROUNDS = TOKEN_TILES // GROUP
+HALVES = N // BANK
+assert GROUP * P == BANK
+STORE = 2
+
+
+def transpose_group(nc, banks, work, identity, rows):
+    words = rows.bitcast(F32).rearrange("r g (p u) -> r g u p", u=2)
+    grouped = work.tile([P, GROUP, P, PACK], BF16, align_bytes=64)
+    grouped_words = grouped[:].bitcast(F32)
+    for first in range(0, GROUP, 2):
+        bank = banks.tile([P, 2, 2, P], F32)
+        for i in range(2):
+            for u in range(2):
+                nc.tensor.transpose(bank[:, i, u, :], words[:, first + i, u, :], identity[:])
+        nc.scalar.copy(
+            out=grouped_words[:, first : first + 2, :, :],
+            in_=bank[:].rearrange("p i u r -> p i r u"),
+        )
+    return grouped
+
+
+def quantise_group(nc, grouped, codes, scales):
+    nc.vector.quantize_mx(
+        out=codes[:].bitcast(FP8X4),
+        scales=scales[:],
+        in_=grouped[:].rearrange("p g r t -> p (g r t)"),
+    )
+
+
+def tile_quantizedlinear_t_kernel(tc, x, weight, alpha, bias, bitwidth, out):
+    assert bitwidth == 2
+    nc = tc.nc
+    x_tiles = x.rearrange("(p j) k -> p j k", j=TOKEN_TILES)
+    out_tiles = out.rearrange("(p j) n -> p j n", j=TOKEN_TILES)
+    weight_tiles = weight.rearrange("(g p) k -> p g k", p=P)
+
+    with ExitStack() as stack:
+        keep = stack.enter_context(tc.tile_pool(name="keep", bufs=1))
+        work = stack.enter_context(tc.tile_pool(name="work", bufs=4))
+        stores = stack.enter_context(tc.tile_pool(name="stores", bufs=6))
+        banks = stack.enter_context(tc.psum_pool(name="banks", bufs=4))
+        sums = stack.enter_context(tc.psum_pool(name="sums", bufs=4))
+
+        alpha_all = keep.tile([P, 1], BF16)
+        nc.sync.dma_start(out=alpha_all[:], in_=alpha.partition_broadcast(P))
+        weight_rows = []
+        for h in range(HALVES):
+            rows = keep.tile([P, GROUP, K], BF16, name="weight_rows%d" % h)
+            nc.sync.dma_start(out=rows[:], in_=weight_tiles[:, h * GROUP : (h + 1) * GROUP, :])
+            weight_rows.append(rows)
+        x_rows = []
+        for r in range(ROUNDS):
+            rows = keep.tile([P, GROUP, K], BF16, name="x_rows%d" % r)
+            nc.sync.dma_start(out=rows[:], in_=x_tiles[:, r * GROUP : (r + 1) * GROUP, :])
+            x_rows.append(rows)
+
+        bias_rows = keep.tile([P, N], BF16)
+        nc.vector.memset(bias_rows[:], 0.0)
+        nc.scalar.dma_start(out=bias_rows[0:1, :], in_=bias.rearrange("(o n) -> o n", o=1))
+        ones = keep.tile([P, P], BF16)
+        nc.vector.memset(ones[:], 1.0)
+        bias_all = keep.tile([P, N], F32)
+        for h in range(HALVES):
+            cols = slice(h * BANK, (h + 1) * BANK)
+            acc = sums.tile([P, BANK], F32)
+            nc.tensor.matmul(acc[:], lhsT=ones[:], rhs=bias_rows[:, cols], start=True, stop=True)
+            nc.scalar.copy(out=bias_all[:, cols], in_=acc[:])
+
+        identity = keep.tile([P, P], F32)
+        make_identity(nc, identity[:])
+
+        abs_alpha = keep.tile([P, 1], F32)
+        nc.vector.scalar_tensor_tensor(
+            out=abs_alpha[:], in0=alpha_all[:], scalar=-1.0, in1=alpha_all[:], op0=ALU.mult, op1=ALU.max
+        )
+        a = keep.tile([P, 1], F32)
+        nc.vector.tensor_scalar_add(out=a[:], in0=abs_alpha[:], scalar1=1e-8)
+        just_above_half = keep.tile([P, 1], F32)
+        nc.vector.tensor_scalar_mul(out=just_above_half[:], in0=abs_alpha[:], scalar1=0.5 * (1.0 + 2.0**-23))
+        threshold = keep.tile([P, 1], F32)
+        nc.vector.scalar_tensor_tensor(
+            out=threshold[:], in0=a[:], scalar=0.5, in1=just_above_half[:], op0=ALU.mult, op1=ALU.max
+        )
+        neg_threshold = keep.tile([P, 1], F32)
+        nc.vector.tensor_scalar_mul(out=neg_threshold[:], in0=threshold[:], scalar1=-1.0)
+
+        w_used = []
+        for h in range(HALVES):
+            w = weight_rows[h][:].rearrange("p g k -> p (g k)")
+            plus = work.tile([P, GROUP * K], BF16)
+            nc.vector.tensor_scalar(
+                out=plus[:], in0=w, scalar1=threshold[:], scalar2=a[:], op0=ALU.is_ge, op1=ALU.mult
+            )
+            minus = work.tile([P, GROUP * K], BF16)
+            nc.vector.tensor_scalar(
+                out=minus[:], in0=w, scalar1=neg_threshold[:], scalar2=a[:], op0=ALU.is_le, op1=ALU.mult
+            )
+            used = keep.tile([P, GROUP, K], BF16, name="w_used%d" % h)
+            nc.vector.tensor_tensor(
+                out=used[:].rearrange("p g k -> p (g k)"), in0=plus[:], in1=minus[:], op=ALU.subtract
+            )
+            w_used.append(used)
+
+        w_codes = [keep.tile([P, BANK], U32, align_bytes=64, name="w_codes%d" % h) for h in range(HALVES)]
+        w_scales = [keep.tile([P, BANK], U8, align_bytes=64, name="w_scales%d" % h) for h in range(HALVES)]
+        x_codes = [keep.tile([P, GROUP * P], U32, align_bytes=64, name="x_codes%d" % r) for r in range(ROUNDS)]
+        x_scales = [keep.tile([P, GROUP * P], U8, align_bytes=64, name="x_scales%d" % r) for r in range(ROUNDS)]
+
+        def multiply(r):
+            for first in range(0, GROUP, STORE):
+                result = stores.tile([P, STORE, N], F32)
+                for i in range(STORE):
+                    tokens = slice((first + i) * P, (first + i + 1) * P)
+                    for h in range(HALVES):
+                        cols = slice(h * BANK, (h + 1) * BANK)
+                        acc = sums.tile([P, BANK], F32)
+                        nc.tensor.matmul_mx(
+                            out=acc[:],
+                            lhsT=x_codes[r][:, tokens].bitcast(FP8X4),
+                            lhsT_scale=x_scales[r][:, tokens],
+                            rhs=w_codes[h][:].bitcast(FP8X4),
+                            rhs_scale=w_scales[h][:],
+                            start=True,
+                            stop=True,
+                        )
+                        nc.vector.tensor_tensor(out=result[:, i, cols], in0=acc[:], in1=bias_all[:, cols], op=ALU.add)
+                j = r * GROUP + first
+                nc.sync.dma_start(out=out_tiles[:, j : j + STORE, :], in_=result[:])
+
+        w_grouped0 = transpose_group(nc, banks, work, identity, w_used[0][:])
+        x_grouped = {0: transpose_group(nc, banks, work, identity, x_rows[0][:])}
+        w_grouped1 = transpose_group(nc, banks, work, identity, w_used[1][:])
+        x_grouped[1] = transpose_group(nc, banks, work, identity, x_rows[1][:])
+        quantise_group(nc, w_grouped0, w_codes[0], w_scales[0])
+        quantise_group(nc, x_grouped[0], x_codes[0], x_scales[0])
+        quantise_group(nc, w_grouped1, w_codes[1], w_scales[1])
+        for r in range(ROUNDS):
+            if r + 2 < ROUNDS:
+                x_grouped[r + 2] = transpose_group(nc, banks, work, identity, x_rows[r + 2][:])
+            if r + 1 < ROUNDS:
+                quantise_group(nc, x_grouped[r + 1], x_codes[r + 1], x_scales[r + 1])
+            multiply(r)

@@ -23,6 +23,8 @@ ROUNDS = TOKEN_TILES // GROUP
 HALVES = N // BANK
 assert GROUP * P == BANK
 STORE = 2
+assert GROUP == 2 * STORE
+SHARE = 3
 
 
 def transpose_group(nc, banks, work, identity, rows):
@@ -59,26 +61,30 @@ def tile_quantizedlinear_t_kernel(tc, x, weight, alpha, bias, bitwidth, out):
     with ExitStack() as stack:
         keep = stack.enter_context(tc.tile_pool(name="keep", bufs=1))
         work = stack.enter_context(tc.tile_pool(name="work", bufs=4))
-        stores = stack.enter_context(tc.tile_pool(name="stores", bufs=6))
+        stores = stack.enter_context(tc.tile_pool(name="stores", bufs=8))
         banks = stack.enter_context(tc.psum_pool(name="banks", bufs=4))
         sums = stack.enter_context(tc.psum_pool(name="sums", bufs=4))
 
         alpha_all = keep.tile([P, 1], BF16)
-        nc.sync.dma_start(out=alpha_all[:], in_=alpha.partition_broadcast(P))
-        weight_rows = []
-        for h in range(HALVES):
-            rows = keep.tile([P, GROUP, K], BF16, name="weight_rows%d" % h)
-            nc.sync.dma_start(out=rows[:], in_=weight_tiles[:, h * GROUP : (h + 1) * GROUP, :])
-            weight_rows.append(rows)
-        x_rows = []
-        for r in range(ROUNDS):
-            rows = keep.tile([P, GROUP, K], BF16, name="x_rows%d" % r)
-            nc.sync.dma_start(out=rows[:], in_=x_tiles[:, r * GROUP : (r + 1) * GROUP, :])
-            x_rows.append(rows)
-
         bias_rows = keep.tile([P, N], BF16)
+        weight_rows = [keep.tile([P, GROUP, K], BF16, name="weight_rows%d" % h) for h in range(HALVES)]
+        x_rows = [keep.tile([P, GROUP, K], BF16, name="x_rows%d" % r) for r in range(ROUNDS)]
+
+        def load_weight(h):
+            nc.sync.dma_start(out=weight_rows[h][:], in_=weight_tiles[:, h * GROUP : (h + 1) * GROUP, :])
+
+        def load_x(r):
+            nc.sync.dma_start(out=x_rows[r][:], in_=x_tiles[:, r * GROUP : (r + 1) * GROUP, :])
+
         nc.vector.memset(bias_rows[:], 0.0)
-        nc.scalar.dma_start(out=bias_rows[0:1, :], in_=bias.rearrange("(o n) -> o n", o=1))
+        nc.sync.dma_start(out=alpha_all[:], in_=alpha.partition_broadcast(P))
+        load_weight(0)
+        nc.sync.dma_start(out=bias_rows[0:1, :], in_=bias.rearrange("(o n) -> o n", o=1))
+        load_x(0)
+        load_weight(1)
+        for r in range(1, ROUNDS):
+            load_x(r)
+
         ones = keep.tile([P, P], BF16)
         nc.vector.memset(ones[:], 1.0)
         bias_all = keep.tile([P, N], F32)
@@ -128,37 +134,43 @@ def tile_quantizedlinear_t_kernel(tc, x, weight, alpha, bias, bitwidth, out):
         x_codes = [keep.tile([P, GROUP * P], U32, align_bytes=64, name="x_codes%d" % r) for r in range(ROUNDS)]
         x_scales = [keep.tile([P, GROUP * P], U8, align_bytes=64, name="x_scales%d" % r) for r in range(ROUNDS)]
 
-        def multiply(r):
-            for first in range(0, GROUP, STORE):
-                result = stores.tile([P, STORE, N], F32)
+        def multiply(r, first):
+            j = r * GROUP + first
+            result = stores.tile([P, STORE, N], F32)
+            for h in range(HALVES):
+                cols = slice(h * BANK, (h + 1) * BANK)
                 for i in range(STORE):
                     tokens = slice((first + i) * P, (first + i + 1) * P)
-                    for h in range(HALVES):
-                        cols = slice(h * BANK, (h + 1) * BANK)
-                        acc = sums.tile([P, BANK], F32)
-                        nc.tensor.matmul_mx(
-                            out=acc[:],
-                            lhsT=x_codes[r][:, tokens].bitcast(FP8X4),
-                            lhsT_scale=x_scales[r][:, tokens],
-                            rhs=w_codes[h][:].bitcast(FP8X4),
-                            rhs_scale=w_scales[h][:],
-                            start=True,
-                            stop=True,
+                    acc = sums.tile([P, BANK], F32)
+                    nc.tensor.matmul_mx(
+                        out=acc[:],
+                        lhsT=x_codes[r][:, tokens].bitcast(FP8X4),
+                        lhsT_scale=x_scales[r][:, tokens],
+                        rhs=w_codes[h][:].bitcast(FP8X4),
+                        rhs_scale=w_scales[h][:],
+                        start=True,
+                        stop=True,
+                    )
+                    if (j + i) % SHARE == SHARE - 1:
+                        nc.scalar.copy(out=result[:, i, cols], in_=acc[:])
+                        nc.gpsimd.tensor_tensor(
+                            out=result[:, i, cols], in0=result[:, i, cols], in1=bias_all[:, cols], op=ALU.add
                         )
+                    else:
                         nc.vector.tensor_tensor(out=result[:, i, cols], in0=acc[:], in1=bias_all[:, cols], op=ALU.add)
-                j = r * GROUP + first
-                nc.sync.dma_start(out=out_tiles[:, j : j + STORE, :], in_=result[:])
+            nc.sync.dma_start(out=out_tiles[:, j : j + STORE, :], in_=result[:])
 
-        w_grouped0 = transpose_group(nc, banks, work, identity, w_used[0][:])
         x_grouped = {0: transpose_group(nc, banks, work, identity, x_rows[0][:])}
+        w_grouped0 = transpose_group(nc, banks, work, identity, w_used[0][:])
         w_grouped1 = transpose_group(nc, banks, work, identity, w_used[1][:])
         x_grouped[1] = transpose_group(nc, banks, work, identity, x_rows[1][:])
-        quantise_group(nc, w_grouped0, w_codes[0], w_scales[0])
         quantise_group(nc, x_grouped[0], x_codes[0], x_scales[0])
+        quantise_group(nc, w_grouped0, w_codes[0], w_scales[0])
         quantise_group(nc, w_grouped1, w_codes[1], w_scales[1])
         for r in range(ROUNDS):
             if r + 2 < ROUNDS:
                 x_grouped[r + 2] = transpose_group(nc, banks, work, identity, x_rows[r + 2][:])
+            multiply(r, 0)
             if r + 1 < ROUNDS:
                 quantise_group(nc, x_grouped[r + 1], x_codes[r + 1], x_scales[r + 1])
-            multiply(r)
+            multiply(r, STORE)

@@ -16,38 +16,38 @@ FLOPS = 2 * T * K * N
 P = 128
 PACK = 4
 assert K == P * PACK
-GROUP = 4
+PAIR = 2
+LOAD = 2
 BANK = 512
-TOKEN_TILES = T // P
-ROUNDS = TOKEN_TILES // GROUP
 HALVES = N // BANK
-assert GROUP * P == BANK
-STORE = 2
-assert GROUP == 2 * STORE
+TOKEN_TILES = T // P
+X_PAIRS = TOKEN_TILES // PAIR
+W_PAIRS = N // (P * PAIR)
+W_PAIRS_IN_HALF = W_PAIRS // HALVES
 SHARE = 3
 
 
-def transpose_group(nc, banks, work, identity, rows):
-    words = rows.bitcast(F32).rearrange("r g (p u) -> r g u p", u=2)
-    grouped = work.tile([P, GROUP, P, PACK], BF16, align_bytes=64)
-    grouped_words = grouped[:].bitcast(F32)
-    for first in range(0, GROUP, 2):
-        bank = banks.tile([P, 2, 2, P], F32)
-        for i in range(2):
-            for u in range(2):
-                nc.tensor.transpose(bank[:, i, u, :], words[:, first + i, u, :], identity[:])
-        nc.scalar.copy(
-            out=grouped_words[:, first : first + 2, :, :],
-            in_=bank[:].rearrange("p i u r -> p i r u"),
-        )
+def pair_of(loads, pair):
+    first = (pair % LOAD) * PAIR
+    return loads[pair // LOAD][:, first : first + PAIR, :]
+
+
+def transpose_pair(nc, banks, work, identity, rows):
+    words = rows.bitcast(F32).rearrange("r i (p u) -> r i u p", u=2)
+    bank = banks.tile([P, PAIR, 2, P], F32)
+    for i in range(PAIR):
+        for u in range(2):
+            nc.tensor.transpose(bank[:, i, u, :], words[:, i, u, :], identity[:])
+    grouped = work.tile([P, PAIR, P, PACK], BF16, align_bytes=64)
+    nc.scalar.copy(out=grouped[:].bitcast(F32), in_=bank[:].rearrange("p i u r -> p i r u"))
     return grouped
 
 
-def quantise_group(nc, grouped, codes, scales):
+def quantise_pair(nc, grouped, codes, scales):
     nc.vector.quantize_mx(
-        out=codes[:].bitcast(FP8X4),
-        scales=scales[:],
-        in_=grouped[:].rearrange("p g r t -> p (g r t)"),
+        out=codes.bitcast(FP8X4),
+        scales=scales,
+        in_=grouped[:].rearrange("p i r t -> p (i r t)"),
     )
 
 
@@ -57,36 +57,51 @@ def tile_quantizedlinear_t_kernel(tc, x, weight, alpha, bias, bitwidth, out):
     x_tiles = x.rearrange("(p j) k -> p j k", j=TOKEN_TILES)
     out_tiles = out.rearrange("(p j) n -> p j n", j=TOKEN_TILES)
     weight_tiles = weight.rearrange("(g p) k -> p g k", p=P)
+    tiles_in_load = LOAD * PAIR
 
     with ExitStack() as stack:
         keep = stack.enter_context(tc.tile_pool(name="keep", bufs=1))
-        work = stack.enter_context(tc.tile_pool(name="work", bufs=4))
+        work = stack.enter_context(tc.tile_pool(name="work", bufs=6))
         stores = stack.enter_context(tc.tile_pool(name="stores", bufs=8))
         banks = stack.enter_context(tc.psum_pool(name="banks", bufs=4))
         sums = stack.enter_context(tc.psum_pool(name="sums", bufs=4))
 
         alpha_all = keep.tile([P, 1], BF16)
         bias_rows = keep.tile([P, N], BF16)
-        weight_rows = [keep.tile([P, GROUP, K], BF16, name="weight_rows%d" % h) for h in range(HALVES)]
-        x_rows = [keep.tile([P, GROUP, K], BF16, name="x_rows%d" % r) for r in range(ROUNDS)]
+        weight_loads = [
+            keep.tile([P, tiles_in_load, K], BF16, name="weight_load%d" % c) for c in range(W_PAIRS // LOAD)
+        ]
+        x_loads = [keep.tile([P, tiles_in_load, K], BF16, name="x_load%d" % c) for c in range(X_PAIRS // LOAD)]
 
-        def load_weight(h):
-            nc.sync.dma_start(out=weight_rows[h][:], in_=weight_tiles[:, h * GROUP : (h + 1) * GROUP, :])
-
-        def load_x(r):
-            nc.sync.dma_start(out=x_rows[r][:], in_=x_tiles[:, r * GROUP : (r + 1) * GROUP, :])
-
-        nc.vector.memset(bias_rows[:], 0.0)
-        nc.sync.dma_start(out=alpha_all[:], in_=alpha.partition_broadcast(P))
-        load_weight(0)
-        nc.sync.dma_start(out=bias_rows[0:1, :], in_=bias.rearrange("(o n) -> o n", o=1))
-        load_x(0)
-        load_weight(1)
-        for r in range(1, ROUNDS):
-            load_x(r)
+        def load(tiles, loads, c):
+            nc.sync.dma_start(out=loads[c][:], in_=tiles[:, c * tiles_in_load : (c + 1) * tiles_in_load, :])
 
         ones = keep.tile([P, P], BF16)
+        nc.vector.memset(bias_rows[:], 0.0)
         nc.vector.memset(ones[:], 1.0)
+        nc.sync.dma_start(out=alpha_all[:], in_=alpha.partition_broadcast(P))
+        load(weight_tiles, weight_loads, 0)
+        nc.sync.dma_start(out=bias_rows[0:1, :], in_=bias.rearrange("(o n) -> o n", o=1))
+        load(x_tiles, x_loads, 0)
+        load(weight_tiles, weight_loads, 1)
+        for c in range(1, X_PAIRS // LOAD):
+            load(x_tiles, x_loads, c)
+
+        abs_alpha = keep.tile([P, 1], F32)
+        nc.vector.scalar_tensor_tensor(
+            out=abs_alpha[:], in0=alpha_all[:], scalar=-1.0, in1=alpha_all[:], op0=ALU.mult, op1=ALU.max
+        )
+        just_above_half = keep.tile([P, 1], F32)
+        nc.vector.tensor_scalar_mul(out=just_above_half[:], in0=abs_alpha[:], scalar1=0.5 * (1.0 + 2.0**-23))
+        a = keep.tile([P, 1], F32)
+        nc.vector.tensor_scalar_add(out=a[:], in0=abs_alpha[:], scalar1=1e-8)
+        threshold = keep.tile([P, 1], F32)
+        nc.vector.scalar_tensor_tensor(
+            out=threshold[:], in0=a[:], scalar=0.5, in1=just_above_half[:], op0=ALU.mult, op1=ALU.max
+        )
+        neg_threshold = keep.tile([P, 1], F32)
+        nc.vector.tensor_scalar_mul(out=neg_threshold[:], in0=threshold[:], scalar1=-1.0)
+
         bias_all = keep.tile([P, N], F32)
         for h in range(HALVES):
             cols = slice(h * BANK, (h + 1) * BANK)
@@ -97,80 +112,70 @@ def tile_quantizedlinear_t_kernel(tc, x, weight, alpha, bias, bitwidth, out):
         identity = keep.tile([P, P], F32)
         make_identity(nc, identity[:])
 
-        abs_alpha = keep.tile([P, 1], F32)
-        nc.vector.scalar_tensor_tensor(
-            out=abs_alpha[:], in0=alpha_all[:], scalar=-1.0, in1=alpha_all[:], op0=ALU.mult, op1=ALU.max
-        )
-        a = keep.tile([P, 1], F32)
-        nc.vector.tensor_scalar_add(out=a[:], in0=abs_alpha[:], scalar1=1e-8)
-        just_above_half = keep.tile([P, 1], F32)
-        nc.vector.tensor_scalar_mul(out=just_above_half[:], in0=abs_alpha[:], scalar1=0.5 * (1.0 + 2.0**-23))
-        threshold = keep.tile([P, 1], F32)
-        nc.vector.scalar_tensor_tensor(
-            out=threshold[:], in0=a[:], scalar=0.5, in1=just_above_half[:], op0=ALU.mult, op1=ALU.max
-        )
-        neg_threshold = keep.tile([P, 1], F32)
-        nc.vector.tensor_scalar_mul(out=neg_threshold[:], in0=threshold[:], scalar1=-1.0)
-
-        w_used = []
-        for h in range(HALVES):
-            w = weight_rows[h][:].rearrange("p g k -> p (g k)")
-            plus = work.tile([P, GROUP * K], BF16)
-            nc.vector.tensor_scalar(
-                out=plus[:], in0=w, scalar1=threshold[:], scalar2=a[:], op0=ALU.is_ge, op1=ALU.mult
-            )
-            minus = work.tile([P, GROUP * K], BF16)
-            nc.vector.tensor_scalar(
-                out=minus[:], in0=w, scalar1=neg_threshold[:], scalar2=a[:], op0=ALU.is_le, op1=ALU.mult
-            )
-            used = keep.tile([P, GROUP, K], BF16, name="w_used%d" % h)
-            nc.vector.tensor_tensor(
-                out=used[:].rearrange("p g k -> p (g k)"), in0=plus[:], in1=minus[:], op=ALU.subtract
-            )
-            w_used.append(used)
-
         w_codes = [keep.tile([P, BANK], U32, align_bytes=64, name="w_codes%d" % h) for h in range(HALVES)]
         w_scales = [keep.tile([P, BANK], U8, align_bytes=64, name="w_scales%d" % h) for h in range(HALVES)]
-        x_codes = [keep.tile([P, GROUP * P], U32, align_bytes=64, name="x_codes%d" % r) for r in range(ROUNDS)]
-        x_scales = [keep.tile([P, GROUP * P], U8, align_bytes=64, name="x_scales%d" % r) for r in range(ROUNDS)]
+        x_codes = [keep.tile([P, PAIR * P], U32, align_bytes=64, name="x_codes%d" % u) for u in range(X_PAIRS)]
+        x_scales = [keep.tile([P, PAIR * P], U8, align_bytes=64, name="x_scales%d" % u) for u in range(X_PAIRS)]
+        x_grouped = {}
 
-        def multiply(r, first):
-            j = r * GROUP + first
-            result = stores.tile([P, STORE, N], F32)
+        def transpose_x(u):
+            x_grouped[u] = transpose_pair(nc, banks, work, identity, pair_of(x_loads, u))
+
+        def quantise_x(u):
+            quantise_pair(nc, x_grouped[u], x_codes[u][:], x_scales[u][:])
+
+        def multiply(u):
+            result = stores.tile([P, PAIR, N], F32)
             for h in range(HALVES):
                 cols = slice(h * BANK, (h + 1) * BANK)
-                for i in range(STORE):
-                    tokens = slice((first + i) * P, (first + i + 1) * P)
+                for i in range(PAIR):
+                    tokens = slice(i * P, (i + 1) * P)
                     acc = sums.tile([P, BANK], F32)
                     nc.tensor.matmul_mx(
                         out=acc[:],
-                        lhsT=x_codes[r][:, tokens].bitcast(FP8X4),
-                        lhsT_scale=x_scales[r][:, tokens],
+                        lhsT=x_codes[u][:, tokens].bitcast(FP8X4),
+                        lhsT_scale=x_scales[u][:, tokens],
                         rhs=w_codes[h][:].bitcast(FP8X4),
                         rhs_scale=w_scales[h][:],
                         start=True,
                         stop=True,
                     )
-                    if (j + i) % SHARE == SHARE - 1:
+                    if (u * PAIR + i) % SHARE == SHARE - 1:
                         nc.scalar.copy(out=result[:, i, cols], in_=acc[:])
                         nc.gpsimd.tensor_tensor(
                             out=result[:, i, cols], in0=result[:, i, cols], in1=bias_all[:, cols], op=ALU.add
                         )
                     else:
                         nc.vector.tensor_tensor(out=result[:, i, cols], in0=acc[:], in1=bias_all[:, cols], op=ALU.add)
-            nc.sync.dma_start(out=out_tiles[:, j : j + STORE, :], in_=result[:])
+                if h == 0 and u + 1 < X_PAIRS:
+                    quantise_x(u + 1)
+            nc.sync.dma_start(out=out_tiles[:, u * PAIR : (u + 1) * PAIR, :], in_=result[:])
 
-        x_grouped = {0: transpose_group(nc, banks, work, identity, x_rows[0][:])}
-        w_grouped0 = transpose_group(nc, banks, work, identity, w_used[0][:])
-        w_grouped1 = transpose_group(nc, banks, work, identity, w_used[1][:])
-        x_grouped[1] = transpose_group(nc, banks, work, identity, x_rows[1][:])
-        quantise_group(nc, x_grouped[0], x_codes[0], x_scales[0])
-        quantise_group(nc, w_grouped0, w_codes[0], w_scales[0])
-        quantise_group(nc, w_grouped1, w_codes[1], w_scales[1])
-        for r in range(ROUNDS):
-            if r + 2 < ROUNDS:
-                x_grouped[r + 2] = transpose_group(nc, banks, work, identity, x_rows[r + 2][:])
-            multiply(r, 0)
-            if r + 1 < ROUNDS:
-                quantise_group(nc, x_grouped[r + 1], x_codes[r + 1], x_scales[r + 1])
-            multiply(r, STORE)
+        transpose_x(0)
+        w_grouped = []
+        for v in range(W_PAIRS):
+            w = pair_of(weight_loads, v).rearrange("p i k -> p (i k)")
+            plus = work.tile([P, PAIR * K], BF16)
+            nc.vector.tensor_scalar(
+                out=plus[:], in0=w, scalar1=threshold[:], scalar2=a[:], op0=ALU.is_ge, op1=ALU.mult
+            )
+            minus = work.tile([P, PAIR * K], BF16)
+            nc.vector.tensor_scalar(
+                out=minus[:], in0=w, scalar1=neg_threshold[:], scalar2=a[:], op0=ALU.is_le, op1=ALU.mult
+            )
+            w_used = work.tile([P, PAIR, K], BF16)
+            nc.vector.tensor_tensor(
+                out=w_used[:].rearrange("p i k -> p (i k)"), in0=plus[:], in1=minus[:], op=ALU.subtract
+            )
+            w_grouped.append(transpose_pair(nc, banks, work, identity, w_used[:]))
+        transpose_x(1)
+        quantise_x(0)
+        for v in range(W_PAIRS):
+            h = v // W_PAIRS_IN_HALF
+            cols = slice((v % W_PAIRS_IN_HALF) * PAIR * P, (v % W_PAIRS_IN_HALF + 1) * PAIR * P)
+            quantise_pair(nc, w_grouped[v], w_codes[h][:, cols], w_scales[h][:, cols])
+
+        for u in range(X_PAIRS):
+            multiply(u)
+            if u + 2 < X_PAIRS:
+                transpose_x(u + 2)

@@ -17,38 +17,24 @@ P = 128
 PACK = 4
 assert K == P * PACK
 PAIR = 2
-LOAD = 2
+X_LOAD_TILES = (4, 4, 8, 8, 8)
 BANK = 512
 HALVES = N // BANK
 TOKEN_TILES = T // P
 X_PAIRS = TOKEN_TILES // PAIR
 W_PAIRS = N // (P * PAIR)
 W_PAIRS_IN_HALF = W_PAIRS // HALVES
+HALF_TILES = W_PAIRS_IN_HALF * PAIR
 SHARE = 3
 
 
-def pair_of(loads, pair):
-    first = (pair % LOAD) * PAIR
-    return loads[pair // LOAD][:, first : first + PAIR, :]
-
-
-def transpose_pair(nc, banks, work, identity, rows):
+def transpose_words(nc, banks, identity, rows):
     words = rows.bitcast(F32).rearrange("r i (p u) -> r i u p", u=2)
     bank = banks.tile([P, PAIR, 2, P], F32)
     for i in range(PAIR):
         for u in range(2):
             nc.tensor.transpose(bank[:, i, u, :], words[:, i, u, :], identity[:])
-    grouped = work.tile([P, PAIR, P, PACK], BF16, align_bytes=64)
-    nc.scalar.copy(out=grouped[:].bitcast(F32), in_=bank[:].rearrange("p i u r -> p i r u"))
-    return grouped
-
-
-def quantise_pair(nc, grouped, codes, scales):
-    nc.vector.quantize_mx(
-        out=codes.bitcast(FP8X4),
-        scales=scales,
-        in_=grouped[:].rearrange("p i r t -> p (i r t)"),
-    )
+    return bank
 
 
 def tile_quantizedlinear_t_kernel(tc, x, weight, alpha, bias, bitwidth, out):
@@ -56,8 +42,7 @@ def tile_quantizedlinear_t_kernel(tc, x, weight, alpha, bias, bitwidth, out):
     nc = tc.nc
     x_tiles = x.rearrange("(p j) k -> p j k", j=TOKEN_TILES)
     out_tiles = out.rearrange("(p j) n -> p j n", j=TOKEN_TILES)
-    weight_tiles = weight.rearrange("(g p) k -> p g k", p=P)
-    tiles_in_load = LOAD * PAIR
+    weight_halves = weight.rearrange("(h p g) k -> h p g k", p=P, g=HALF_TILES)
 
     with ExitStack() as stack:
         keep = stack.enter_context(tc.tile_pool(name="keep", bufs=1))
@@ -68,24 +53,30 @@ def tile_quantizedlinear_t_kernel(tc, x, weight, alpha, bias, bitwidth, out):
 
         alpha_all = keep.tile([P, 1], BF16)
         bias_rows = keep.tile([P, N], BF16)
-        weight_loads = [
-            keep.tile([P, tiles_in_load, K], BF16, name="weight_load%d" % c) for c in range(W_PAIRS // LOAD)
-        ]
-        x_loads = [keep.tile([P, tiles_in_load, K], BF16, name="x_load%d" % c) for c in range(X_PAIRS // LOAD)]
+        weight_loads = [keep.tile([P, HALF_TILES, K], BF16, name="weight_load%d" % h) for h in range(HALVES)]
+        x_loads = [keep.tile([P, w, K], BF16, name="x_load%d" % c) for c, w in enumerate(X_LOAD_TILES)]
+        x_pairs = []
 
-        def load(tiles, loads, c):
-            nc.sync.dma_start(out=loads[c][:], in_=tiles[:, c * tiles_in_load : (c + 1) * tiles_in_load, :])
+        def load_weight(h):
+            nc.sync.dma_start(out=weight_loads[h][:], in_=weight_halves[h])
+
+        def load_x(c):
+            first = len(x_pairs) * PAIR
+            width = X_LOAD_TILES[c]
+            nc.sync.dma_start(out=x_loads[c][:], in_=x_tiles[:, first : first + width, :])
+            x_pairs.extend([x_loads[c][:, i : i + PAIR, :] for i in range(0, width, PAIR)])
 
         ones = keep.tile([P, P], BF16)
         nc.vector.memset(bias_rows[:], 0.0)
         nc.vector.memset(ones[:], 1.0)
         nc.sync.dma_start(out=alpha_all[:], in_=alpha.partition_broadcast(P))
-        load(weight_tiles, weight_loads, 0)
+        load_weight(0)
         nc.sync.dma_start(out=bias_rows[0:1, :], in_=bias.rearrange("(o n) -> o n", o=1))
-        load(x_tiles, x_loads, 0)
-        load(weight_tiles, weight_loads, 1)
-        for c in range(1, X_PAIRS // LOAD):
-            load(x_tiles, x_loads, c)
+        load_x(0)
+        load_weight(1)
+        for c in range(1, len(X_LOAD_TILES)):
+            load_x(c)
+        assert len(x_pairs) == X_PAIRS
 
         abs_alpha = keep.tile([P, 1], F32)
         nc.vector.scalar_tensor_tensor(
@@ -119,10 +110,17 @@ def tile_quantizedlinear_t_kernel(tc, x, weight, alpha, bias, bitwidth, out):
         x_grouped = {}
 
         def transpose_x(u):
-            x_grouped[u] = transpose_pair(nc, banks, work, identity, pair_of(x_loads, u))
+            bank = transpose_words(nc, banks, identity, x_pairs[u])
+            grouped = work.tile([P, PAIR, P, PACK], BF16, align_bytes=64)
+            nc.scalar.copy(out=grouped[:].bitcast(F32), in_=bank[:].rearrange("p i u r -> p i r u"))
+            x_grouped[u] = grouped
 
         def quantise_x(u):
-            quantise_pair(nc, x_grouped[u], x_codes[u][:], x_scales[u][:])
+            nc.vector.quantize_mx(
+                out=x_codes[u][:].bitcast(FP8X4),
+                scales=x_scales[u][:],
+                in_=x_grouped[u][:].rearrange("p i r t -> p (i r t)"),
+            )
 
         def multiply(u):
             result = stores.tile([P, PAIR, N], F32)
@@ -152,9 +150,11 @@ def tile_quantizedlinear_t_kernel(tc, x, weight, alpha, bias, bitwidth, out):
             nc.sync.dma_start(out=out_tiles[:, u * PAIR : (u + 1) * PAIR, :], in_=result[:])
 
         transpose_x(0)
-        w_grouped = []
+        w_grouped = [keep.tile([P, BANK, PACK], BF16, align_bytes=64, name="w_grouped%d" % h) for h in range(HALVES)]
         for v in range(W_PAIRS):
-            w = pair_of(weight_loads, v).rearrange("p i k -> p (i k)")
+            h = v // W_PAIRS_IN_HALF
+            q = v % W_PAIRS_IN_HALF
+            w = weight_loads[h][:, q * PAIR : (q + 1) * PAIR, :].rearrange("p i k -> p (i k)")
             plus = work.tile([P, PAIR * K], BF16)
             nc.vector.tensor_scalar(
                 out=plus[:], in0=w, scalar1=threshold[:], scalar2=a[:], op0=ALU.is_ge, op1=ALU.mult
@@ -167,13 +167,20 @@ def tile_quantizedlinear_t_kernel(tc, x, weight, alpha, bias, bitwidth, out):
             nc.vector.tensor_tensor(
                 out=w_used[:].rearrange("p i k -> p (i k)"), in0=plus[:], in1=minus[:], op=ALU.subtract
             )
-            w_grouped.append(transpose_pair(nc, banks, work, identity, w_used[:]))
+            bank = transpose_words(nc, banks, identity, w_used[:])
+            words = w_grouped[h][:].rearrange("p f t -> p (f t)").bitcast(F32)
+            nc.scalar.copy(
+                out=words.rearrange("p (r q i u) -> p q r i u", q=W_PAIRS_IN_HALF, i=PAIR, u=2)[:, q],
+                in_=bank[:].rearrange("p i u r -> p r i u"),
+            )
         transpose_x(1)
         quantise_x(0)
-        for v in range(W_PAIRS):
-            h = v // W_PAIRS_IN_HALF
-            cols = slice((v % W_PAIRS_IN_HALF) * PAIR * P, (v % W_PAIRS_IN_HALF + 1) * PAIR * P)
-            quantise_pair(nc, w_grouped[v], w_codes[h][:, cols], w_scales[h][:, cols])
+        for h in range(HALVES):
+            nc.vector.quantize_mx(
+                out=w_codes[h][:].bitcast(FP8X4),
+                scales=w_scales[h][:],
+                in_=w_grouped[h][:].rearrange("p f t -> p (f t)"),
+            )
 
         for u in range(X_PAIRS):
             multiply(u)

@@ -26,6 +26,7 @@ W_PAIRS = N // (P * PAIR)
 W_PAIRS_IN_HALF = W_PAIRS // HALVES
 HALF_TILES = W_PAIRS_IN_HALF * PAIR
 SHARE = 3
+X_BATCHES = [(0,), (1,)] + [(u, u + 1) for u in range(2, X_PAIRS, 2)]
 
 
 def transpose_words(nc, banks, identity, rows):
@@ -105,21 +106,32 @@ def tile_quantizedlinear_t_kernel(tc, x, weight, alpha, bias, bitwidth, out):
 
         w_codes = [keep.tile([P, BANK], U32, align_bytes=64, name="w_codes%d" % h) for h in range(HALVES)]
         w_scales = [keep.tile([P, BANK], U8, align_bytes=64, name="w_scales%d" % h) for h in range(HALVES)]
-        x_codes = [keep.tile([P, PAIR * P], U32, align_bytes=64, name="x_codes%d" % u) for u in range(X_PAIRS)]
-        x_scales = [keep.tile([P, PAIR * P], U8, align_bytes=64, name="x_scales%d" % u) for u in range(X_PAIRS)]
+        x_codes = []
+        x_scales = []
+        batch_of = {}
+        for b, batch in enumerate(X_BATCHES):
+            x_codes.append(keep.tile([P, len(batch) * PAIR * P], U32, align_bytes=64, name="x_codes%d" % b))
+            x_scales.append(keep.tile([P, len(batch) * PAIR * P], U8, align_bytes=64, name="x_scales%d" % b))
+            for u in batch:
+                batch_of[u] = b
         x_grouped = {}
 
         def transpose_x(u):
+            b = batch_of[u]
+            if b not in x_grouped:
+                x_grouped[b] = work.tile([P, len(X_BATCHES[b]) * PAIR, P, PACK], BF16, align_bytes=64, name="x_grouped")
+            s = u - X_BATCHES[b][0]
             bank = transpose_words(nc, banks, identity, x_pairs[u])
-            grouped = work.tile([P, PAIR, P, PACK], BF16, align_bytes=64)
-            nc.scalar.copy(out=grouped[:].bitcast(F32), in_=bank[:].rearrange("p i u r -> p i r u"))
-            x_grouped[u] = grouped
+            nc.scalar.copy(
+                out=x_grouped[b][:, s * PAIR : (s + 1) * PAIR, :, :].bitcast(F32),
+                in_=bank[:].rearrange("p i u r -> p i r u"),
+            )
 
-        def quantise_x(u):
+        def quantise_x(b):
             nc.vector.quantize_mx(
-                out=x_codes[u][:].bitcast(FP8X4),
-                scales=x_scales[u][:],
-                in_=x_grouped[u][:].rearrange("p i r t -> p (i r t)"),
+                out=x_codes[b][:].bitcast(FP8X4),
+                scales=x_scales[b][:],
+                in_=x_grouped[b][:].rearrange("p i r t -> p (i r t)"),
             )
 
         def multiply(u):
@@ -127,12 +139,14 @@ def tile_quantizedlinear_t_kernel(tc, x, weight, alpha, bias, bitwidth, out):
             for h in range(HALVES):
                 cols = slice(h * BANK, (h + 1) * BANK)
                 for i in range(PAIR):
-                    tokens = slice(i * P, (i + 1) * P)
+                    b = batch_of[u]
+                    column = ((u - X_BATCHES[b][0]) * PAIR + i) * P
+                    tokens = slice(column, column + P)
                     acc = sums.tile([P, BANK], F32)
                     nc.tensor.matmul_mx(
                         out=acc[:],
-                        lhsT=x_codes[u][:, tokens].bitcast(FP8X4),
-                        lhsT_scale=x_scales[u][:, tokens],
+                        lhsT=x_codes[b][:, tokens].bitcast(FP8X4),
+                        lhsT_scale=x_scales[b][:, tokens],
                         rhs=w_codes[h][:].bitcast(FP8X4),
                         rhs_scale=w_scales[h][:],
                         start=True,
@@ -145,8 +159,8 @@ def tile_quantizedlinear_t_kernel(tc, x, weight, alpha, bias, bitwidth, out):
                         )
                     else:
                         nc.vector.tensor_tensor(out=result[:, i, cols], in0=acc[:], in1=bias_all[:, cols], op=ALU.add)
-                if h == 0 and u + 1 < X_PAIRS:
-                    quantise_x(u + 1)
+                if h == 0 and u + 1 < X_PAIRS and X_BATCHES[batch_of[u + 1]][0] == u + 1:
+                    quantise_x(batch_of[u + 1])
             nc.sync.dma_start(out=out_tiles[:, u * PAIR : (u + 1) * PAIR, :], in_=result[:])
 
         transpose_x(0)
@@ -184,5 +198,6 @@ def tile_quantizedlinear_t_kernel(tc, x, weight, alpha, bias, bitwidth, out):
 
         for u in range(X_PAIRS):
             multiply(u)
-            if u + 2 < X_PAIRS:
-                transpose_x(u + 2)
+            for ahead in (2, 3) if u == 0 else (3,):
+                if u + ahead < X_PAIRS:
+                    transpose_x(u + ahead)

@@ -26,6 +26,8 @@ W_PAIRS = N // (P * PAIR)
 W_PAIRS_IN_HALF = W_PAIRS // HALVES
 HALF_TILES = W_PAIRS_IN_HALF * PAIR
 SHARE = 3
+SHARE_FROM = 3
+HEAD_PAIRS = 6
 X_BATCHES = [(0,), (1,)] + [(u, u + 1) for u in range(2, X_PAIRS, 2)]
 
 
@@ -51,6 +53,7 @@ def tile_quantizedlinear_t_kernel(tc, x, weight, alpha, bias, bitwidth, out):
         stores = stack.enter_context(tc.tile_pool(name="stores", bufs=8))
         banks = stack.enter_context(tc.psum_pool(name="banks", bufs=4))
         sums = stack.enter_context(tc.psum_pool(name="sums", bufs=4))
+        stack.enter_context(tc.manual_schedule(engines={mybir.EngineType.SP}))
 
         alpha_all = keep.tile([P, 1], BF16)
         bias_rows = keep.tile([P, N], BF16)
@@ -134,34 +137,61 @@ def tile_quantizedlinear_t_kernel(tc, x, weight, alpha, bias, bitwidth, out):
                 in_=x_grouped[b][:].rearrange("p i r t -> p (i r t)"),
             )
 
+        def on_gpsimd(u, i):
+            tile_index = u * PAIR + i
+            return tile_index >= SHARE_FROM and tile_index % SHARE == SHARE_FROM % SHARE
+
+        def multiply_part(result, u, i, h):
+            cols = slice(h * BANK, (h + 1) * BANK)
+            b = batch_of[u]
+            column = ((u - X_BATCHES[b][0]) * PAIR + i) * P
+            tokens = slice(column, column + P)
+            acc = sums.tile([P, BANK], F32, name="acc")
+            nc.tensor.matmul_mx(
+                out=acc[:],
+                lhsT=x_codes[b][:, tokens].bitcast(FP8X4),
+                lhsT_scale=x_scales[b][:, tokens],
+                rhs=w_codes[h][:].bitcast(FP8X4),
+                rhs_scale=w_scales[h][:],
+                start=True,
+                stop=True,
+            )
+            if on_gpsimd(u, i):
+                nc.scalar.copy(out=result[:, i, cols], in_=acc[:])
+                nc.gpsimd.tensor_tensor(
+                    out=result[:, i, cols], in0=result[:, i, cols], in1=bias_all[:, cols], op=ALU.add
+                )
+            else:
+                nc.vector.tensor_tensor(out=result[:, i, cols], in0=acc[:], in1=bias_all[:, cols], op=ALU.add)
+
+        waiting = []
+
+        def store_tiles(tiles):
+            for j, tile_result in tiles:
+                nc.sync.dma_start(out=out_tiles[:, j, :], in_=tile_result)
+
         def multiply(u):
-            result = stores.tile([P, PAIR, N], F32)
-            for h in range(HALVES):
-                cols = slice(h * BANK, (h + 1) * BANK)
-                for i in range(PAIR):
-                    b = batch_of[u]
-                    column = ((u - X_BATCHES[b][0]) * PAIR + i) * P
-                    tokens = slice(column, column + P)
-                    acc = sums.tile([P, BANK], F32)
-                    nc.tensor.matmul_mx(
-                        out=acc[:],
-                        lhsT=x_codes[b][:, tokens].bitcast(FP8X4),
-                        lhsT_scale=x_scales[b][:, tokens],
-                        rhs=w_codes[h][:].bitcast(FP8X4),
-                        rhs_scale=w_scales[h][:],
-                        start=True,
-                        stop=True,
-                    )
-                    if (u * PAIR + i) % SHARE == SHARE - 1:
-                        nc.scalar.copy(out=result[:, i, cols], in_=acc[:])
-                        nc.gpsimd.tensor_tensor(
-                            out=result[:, i, cols], in0=result[:, i, cols], in1=bias_all[:, cols], op=ALU.add
-                        )
-                    else:
-                        nc.vector.tensor_tensor(out=result[:, i, cols], in0=acc[:], in1=bias_all[:, cols], op=ALU.add)
-                if h == 0 and u + 1 < X_PAIRS and X_BATCHES[batch_of[u + 1]][0] == u + 1:
+            result = stores.tile([P, PAIR, N], F32, name="result")
+            tiles = sorted(range(PAIR), key=lambda i: not on_gpsimd(u, i))
+            if on_gpsimd(u, tiles[0]) or u >= HEAD_PAIRS:
+                parts = [(i, h) for h in range(HALVES) for i in tiles]
+            else:
+                parts = [(i, h) for i in tiles for h in range(HALVES)]
+            for n, (i, h) in enumerate(parts):
+                multiply_part(result, u, i, h)
+                if n == 1 and u + 1 < X_PAIRS and X_BATCHES[batch_of[u + 1]][0] == u + 1:
                     quantise_x(batch_of[u + 1])
-            nc.sync.dma_start(out=out_tiles[:, u * PAIR : (u + 1) * PAIR, :], in_=result[:])
+            late, waiting[:] = waiting[:], []
+            if u < HEAD_PAIRS:
+                for i in range(PAIR):
+                    if on_gpsimd(u, i):
+                        waiting.append((u * PAIR + i, result[:, i, :]))
+                    else:
+                        store_tiles([(u * PAIR + i, result[:, i, :])] + late)
+                        late = []
+            else:
+                store_tiles(late)
+                nc.sync.dma_start(out=out_tiles[:, u * PAIR : (u + 1) * PAIR, :], in_=result[:])
 
         transpose_x(0)
         w_grouped = [keep.tile([P, BANK, PACK], BF16, align_bytes=64, name="w_grouped%d" % h) for h in range(HALVES)]

@@ -32,7 +32,7 @@ X_BATCHES = [(0,), (1,)] + [(u, u + 1) for u in range(2, X_PAIRS, 2)]
 
 
 def transpose_words(nc, banks, identity, rows):
-    words = rows.bitcast(F32).rearrange("r i (p u) -> r i u p", u=2)
+    words = rows.bitcast(F32).rearrange("r i (u p) -> r i u p", u=2)
     bank = banks.tile([P, PAIR, 2, P], F32)
     for i in range(PAIR):
         for u in range(2):

from contextlib import ExitStack

import concourse.mybir as mybir
from concourse.masks import make_identity

F32 = mybir.dt.float32
BF16 = mybir.dt.bfloat16
U32 = mybir.dt.uint32
U8 = mybir.dt.uint8
FP8X4 = mybir.dt.float8_e4m3fn_x4
ALU = mybir.AluOpType

T, K, N = 4096, 512, 1024
FLOPS = 2 * T * K * N

P = 128
PACK = 4
assert K == P * PACK
PAIR = 2
X_LOAD_TILES = (4, 4, 8, 8, 8)
BANK = 512
HALVES = N // BANK
TOKEN_TILES = T // P
X_PAIRS = TOKEN_TILES // PAIR
W_PAIRS = N // (P * PAIR)
W_PAIRS_IN_HALF = W_PAIRS // HALVES
HALF_TILES = W_PAIRS_IN_HALF * PAIR
SHARE = 3
SHARE_FROM = 3
HEAD_PAIRS = 6
X_BATCHES = [(0,), (1,)] + [(u, u + 1) for u in range(2, X_PAIRS, 2)]


def transpose_words(nc, banks, identity, rows):
    words = rows.bitcast(F32).rearrange("r i (u p) -> r i u p", u=2)
    bank = banks.tile([P, PAIR, 2, P], F32)
    for i in range(PAIR):
        for u in range(2):
            nc.tensor.transpose(bank[:, i, u, :], words[:, i, u, :], identity[:])
    return bank


def tile_quantizedlinear_t_kernel(tc, x, weight, alpha, bias, bitwidth, out):
    assert bitwidth == 2
    nc = tc.nc
    x_tiles = x.rearrange("(p j) k -> p j k", j=TOKEN_TILES)
    out_tiles = out.rearrange("(p j) n -> p j n", j=TOKEN_TILES)
    weight_halves = weight.rearrange("(h p g) k -> h p g k", p=P, g=HALF_TILES)

    with ExitStack() as stack:
        keep = stack.enter_context(tc.tile_pool(name="keep", bufs=1))
        work = stack.enter_context(tc.tile_pool(name="work", bufs=6))
        stores = stack.enter_context(tc.tile_pool(name="stores", bufs=8))
        banks = stack.enter_context(tc.psum_pool(name="banks", bufs=4))
        sums = stack.enter_context(tc.psum_pool(name="sums", bufs=4))
        stack.enter_context(tc.manual_schedule(engines={mybir.EngineType.SP}))

        alpha_all = keep.tile([P, 1], BF16)
        bias_rows = keep.tile([P, N], BF16)
        weight_loads = [keep.tile([P, HALF_TILES, K], BF16, name="weight_load%d" % h) for h in range(HALVES)]
        x_loads = [keep.tile([P, w, K], BF16, name="x_load%d" % c) for c, w in enumerate(X_LOAD_TILES)]
        x_pairs = []

        def load_weight(h):
            nc.sync.dma_start(out=weight_loads[h][:], in_=weight_halves[h])

        def load_x(c):
            first = len(x_pairs) * PAIR
            width = X_LOAD_TILES[c]
            nc.sync.dma_start(out=x_loads[c][:], in_=x_tiles[:, first : first + width, :])
            x_pairs.extend([x_loads[c][:, i : i + PAIR, :] for i in range(0, width, PAIR)])

        ones = keep.tile([P, P], BF16)
        nc.vector.memset(bias_rows[:], 0.0)
        nc.vector.memset(ones[:], 1.0)
        nc.sync.dma_start(out=alpha_all[:], in_=alpha.partition_broadcast(P))
        load_weight(0)
        nc.sync.dma_start(out=bias_rows[0:1, :], in_=bias.rearrange("(o n) -> o n", o=1))
        load_x(0)
        load_weight(1)
        for c in range(1, len(X_LOAD_TILES)):
            load_x(c)
        assert len(x_pairs) == X_PAIRS

        abs_alpha = keep.tile([P, 1], F32)
        nc.vector.scalar_tensor_tensor(
            out=abs_alpha[:], in0=alpha_all[:], scalar=-1.0, in1=alpha_all[:], op0=ALU.mult, op1=ALU.max
        )
        just_above_half = keep.tile([P, 1], F32)
        nc.vector.tensor_scalar_mul(out=just_above_half[:], in0=abs_alpha[:], scalar1=0.5 * (1.0 + 2.0**-23))
        a = keep.tile([P, 1], F32)
        nc.vector.tensor_scalar_add(out=a[:], in0=abs_alpha[:], scalar1=1e-8)
        threshold = keep.tile([P, 1], F32)
        nc.vector.scalar_tensor_tensor(
            out=threshold[:], in0=a[:], scalar=0.5, in1=just_above_half[:], op0=ALU.mult, op1=ALU.max
        )
        neg_threshold = keep.tile([P, 1], F32)
        nc.vector.tensor_scalar_mul(out=neg_threshold[:], in0=threshold[:], scalar1=-1.0)

        bias_all = keep.tile([P, N], F32)
        for h in range(HALVES):
            cols = slice(h * BANK, (h + 1) * BANK)
            acc = sums.tile([P, BANK], F32)
            nc.tensor.matmul(acc[:], lhsT=ones[:], rhs=bias_rows[:, cols], start=True, stop=True)
            nc.scalar.copy(out=bias_all[:, cols], in_=acc[:])

        identity = keep.tile([P, P], F32)
        make_identity(nc, identity[:])

        w_codes = [keep.tile([P, BANK], U32, align_bytes=64, name="w_codes%d" % h) for h in range(HALVES)]
        w_scales = [keep.tile([P, BANK], U8, align_bytes=64, name="w_scales%d" % h) for h in range(HALVES)]
        x_codes = []
        x_scales = []
        batch_of = {}
        for b, batch in enumerate(X_BATCHES):
            x_codes.append(keep.tile([P, len(batch) * PAIR * P], U32, align_bytes=64, name="x_codes%d" % b))
            x_scales.append(keep.tile([P, len(batch) * PAIR * P], U8, align_bytes=64, name="x_scales%d" % b))
            for u in batch:
                batch_of[u] = b
        x_grouped = {}

        def transpose_x(u):
            b = batch_of[u]
            if b not in x_grouped:
                x_grouped[b] = work.tile([P, len(X_BATCHES[b]) * PAIR, P, PACK], BF16, align_bytes=64, name="x_grouped")
            s = u - X_BATCHES[b][0]
            bank = transpose_words(nc, banks, identity, x_pairs[u])
            nc.scalar.copy(
                out=x_grouped[b][:, s * PAIR : (s + 1) * PAIR, :, :].bitcast(F32),
                in_=bank[:].rearrange("p i u r -> p i r u"),
            )

        def quantise_x(b):
            nc.vector.quantize_mx(
                out=x_codes[b][:].bitcast(FP8X4),
                scales=x_scales[b][:],
                in_=x_grouped[b][:].rearrange("p i r t -> p (i r t)"),
            )

        def on_gpsimd(u, i):
            tile_index = u * PAIR + i
            return tile_index >= SHARE_FROM and tile_index % SHARE == SHARE_FROM % SHARE

        def multiply_part(result, u, i, h):
            cols = slice(h * BANK, (h + 1) * BANK)
            b = batch_of[u]
            column = ((u - X_BATCHES[b][0]) * PAIR + i) * P
            tokens = slice(column, column + P)
            acc = sums.tile([P, BANK], F32, name="acc")
            nc.tensor.matmul_mx(
                out=acc[:],
                lhsT=x_codes[b][:, tokens].bitcast(FP8X4),
                lhsT_scale=x_scales[b][:, tokens],
                rhs=w_codes[h][:].bitcast(FP8X4),
                rhs_scale=w_scales[h][:],
                start=True,
                stop=True,
            )
            if on_gpsimd(u, i):
                nc.scalar.copy(out=result[:, i, cols], in_=acc[:])
                nc.gpsimd.tensor_tensor(
                    out=result[:, i, cols], in0=result[:, i, cols], in1=bias_all[:, cols], op=ALU.add
                )
            else:
                nc.vector.tensor_tensor(out=result[:, i, cols], in0=acc[:], in1=bias_all[:, cols], op=ALU.add)

        waiting = []

        def store_tiles(tiles):
            for j, tile_result in tiles:
                nc.sync.dma_start(out=out_tiles[:, j, :], in_=tile_result)

        def multiply(u):
            result = stores.tile([P, PAIR, N], F32, name="result")
            tiles = sorted(range(PAIR), key=lambda i: not on_gpsimd(u, i))
            if on_gpsimd(u, tiles[0]) or u >= HEAD_PAIRS:
                parts = [(i, h) for h in range(HALVES) for i in tiles]
            else:
                parts = [(i, h) for i in tiles for h in range(HALVES)]
            for n, (i, h) in enumerate(parts):
                multiply_part(result, u, i, h)
                if n == 1 and u + 1 < X_PAIRS and X_BATCHES[batch_of[u + 1]][0] == u + 1:
                    quantise_x(batch_of[u + 1])
            late, waiting[:] = waiting[:], []
            if u < HEAD_PAIRS:
                for i in range(PAIR):
                    if on_gpsimd(u, i):
                        waiting.append((u * PAIR + i, result[:, i, :]))
                    else:
                        store_tiles([(u * PAIR + i, result[:, i, :])] + late)
                        late = []
            else:
                store_tiles(late)
                nc.sync.dma_start(out=out_tiles[:, u * PAIR : (u + 1) * PAIR, :], in_=result[:])

        transpose_x(0)
        w_grouped = [keep.tile([P, BANK, PACK], BF16, align_bytes=64, name="w_grouped%d" % h) for h in range(HALVES)]
        for v in range(W_PAIRS):
            h = v // W_PAIRS_IN_HALF
            q = v % W_PAIRS_IN_HALF
            w = weight_loads[h][:, q * PAIR : (q + 1) * PAIR, :].rearrange("p i k -> p (i k)")
            plus = work.tile([P, PAIR * K], BF16)
            nc.vector.tensor_scalar(
                out=plus[:], in0=w, scalar1=threshold[:], scalar2=a[:], op0=ALU.is_ge, op1=ALU.mult
            )
            minus = work.tile([P, PAIR * K], BF16)
            nc.vector.tensor_scalar(
                out=minus[:], in0=w, scalar1=neg_threshold[:], scalar2=a[:], op0=ALU.is_le, op1=ALU.mult
            )
            w_used = work.tile([P, PAIR, K], BF16)
            nc.vector.tensor_tensor(
                out=w_used[:].rearrange("p i k -> p (i k)"), in0=plus[:], in1=minus[:], op=ALU.subtract
            )
            bank = transpose_words(nc, banks, identity, w_used[:])
            words = w_grouped[h][:].rearrange("p f t -> p (f t)").bitcast(F32)
            nc.scalar.copy(
                out=words.rearrange("p (r q i u) -> p q r i u", q=W_PAIRS_IN_HALF, i=PAIR, u=2)[:, q],
                in_=bank[:].rearrange("p i u r -> p r i u"),
            )
        transpose_x(1)
        quantise_x(0)
        for h in range(HALVES):
            nc.vector.quantize_mx(
                out=w_codes[h][:].bitcast(FP8X4),
                scales=w_scales[h][:],
                in_=w_grouped[h][:].rearrange("p f t -> p (f t)"),
            )

        for u in range(X_PAIRS):
            multiply(u)
            for ahead in (2, 3) if u == 0 else (3,):
                if u + ahead < X_PAIRS:
                    transpose_x(u + ahead)
